import numpy as np
import ml_dtypes


def mxq(x, axis, fmt="e4m3"):
    dtype, down = {"e4m3": (ml_dtypes.float8_e4m3fn, 7), "e5m2": (ml_dtypes.float8_e5m2, 14)}[fmt]
    v = np.moveaxis(np.asarray(x, np.float32).astype(ml_dtypes.bfloat16).astype(np.float64), axis, -1)
    blocks = v.reshape(v.shape[:-1] + (-1, 32))
    amax = np.abs(blocks).max(-1, keepdims=True)
    byte = np.maximum(np.where(amax > 0, np.frexp(amax)[1] - 1 + 127, 0) - down, 1)
    scale = np.exp2(byte - 127.0)
    codes = (blocks / scale).astype(np.float32).astype(dtype).astype(np.float64)
    return np.moveaxis((codes * scale).reshape(v.shape), -1, axis)


WIDE = False


def mx_kscale(k):
    if not WIDE:
        return np.ones(k)
    levels = np.array([20, -20, 10, -10, 0])
    a = np.random.permutation(np.resize(levels, k // 512 * 4)).reshape(k // 512, 4)
    idx = np.arange(k)
    return np.exp2(a[idx // 512, idx % 128 // 32])


BF16 = ml_dtypes.bfloat16


def bf(x):
    return np.asarray(x, np.float32).astype(BF16)


def f64(x):
    return np.asarray(x).astype(np.float64)


B, NQ = 4096, 10
CONTROL = 0
DIM = 1 << NQ
HALF = DIM // 2


def setup_inputs():
    on = np.nonzero((np.arange(DIM) & (1 << (NQ - CONTROL - 1))) != 0)[0]
    uv = np.ones(DIM)
    uv[on] = mx_kscale(HALF)
    state = np.random.standard_normal((B, DIM))
    target_matrix = np.random.standard_normal((DIM, DIM)) / np.sqrt(HALF) / uv[None, :]
    g = np.random.standard_normal((B, DIM)) * np.exp2(np.random.randint(-12, 1, (B, 1))) * 4.0 * uv[None, :]
    return {"state": bf(state),
            "target_matrix": bf(target_matrix),
            "control": CONTROL,
            "num_qubits": NQ,
            "grad_out": bf(g)}


def reference(state, target_matrix, control, num_qubits, grad_out):
    dim = 1 << num_qubits
    mask = 1 << (num_qubits - control - 1)
    c1_mask = (np.arange(dim) & mask) != 0
    on = np.nonzero(c1_mask)[0]
    g, tm = f64(grad_out), f64(target_matrix)
    gs = g.copy()
    gs[:, on] = mxq(g[:, on], 1, "e5m2") @ mxq(tm[np.ix_(on, on)], 1, "e4m3").T
    return gs

@@ -1,0 +1,114 @@
+from contextlib import ExitStack
+
+import concourse.mybir as mybir
+from concourse.masks import make_identity
+
+BF16 = mybir.dt.bfloat16
+F32 = mybir.dt.float32
+U32 = mybir.dt.uint32
+U8 = mybir.dt.uint8
+E5M2_X4 = mybir.dt.float8_e5m2_x4
+E4M3_X4 = mybir.dt.float8_e4m3fn_x4
+
+P = 128
+PACK = 4
+PAIR = 2
+BATCH = 4096
+DIM = 1024
+HALF = DIM // 2
+QUAD = 4
+BANK_ROW_TILES = 2
+
+ROWS_PER_PARTITION = 8
+CHUNKS = BATCH // (P * ROWS_PER_PARTITION)
+
+FLOPS = 2 * BATCH * HALF * HALF
+BYTES = BATCH * DIM * 2 + HALF * HALF * 2 + BATCH * DIM * 4
+
+
+def quantise_four_row_tiles(nc, stage, flip_psum, identity, rows, codes, scales, fp8_x4):
+    grouped = stage.tile([P, QUAD * P * PACK], BF16, align_bytes=64)
+    grouped_words = grouped[:].bitcast(F32).rearrange(
+        "q (s r u) -> q s r u", s=QUAD, r=P, u=PAIR
+    )
+    for first in range(0, QUAD, BANK_ROW_TILES):
+        flipped = flip_psum.tile([P, BANK_ROW_TILES, PAIR, P], F32)
+        for i in range(BANK_ROW_TILES):
+            words = rows[:, first + i, :].bitcast(F32).rearrange("r (q u) -> r u q", u=PAIR)
+            for u in range(PAIR):
+                nc.tensor.transpose(flipped[:, i, u, :], words[:, u, :], identity)
+        nc.vector.tensor_copy(
+            out=grouped_words[:, first : first + BANK_ROW_TILES, :, :],
+            in_=flipped[:].rearrange("q i u r -> q i r u"),
+        )
+    nc.vector.quantize_mx(out=codes.bitcast(fp8_x4), scales=scales, in_=grouped[:])
+
+
+def tile_builtcontrolled_t_kernel(
+    tc, state, target_matrix, control, num_qubits, grad_out, out
+):
+    nc = tc.nc
+    assert control == 0 and num_qubits == 10
+
+    with ExitStack() as ctx:
+        const = ctx.enter_context(tc.tile_pool(name="const", bufs=1))
+        loads = ctx.enter_context(tc.tile_pool(name="loads", bufs=CHUNKS))
+        results = ctx.enter_context(tc.tile_pool(name="results", bufs=CHUNKS))
+        stage = ctx.enter_context(tc.tile_pool(name="stage", bufs=3))
+        flip_psum = ctx.enter_context(tc.psum_pool(name="flip_psum", bufs=4))
+        product_psum = ctx.enter_context(tc.psum_pool(name="product_psum", bufs=4))
+
+        w_rows = const.tile([P, QUAD, HALF], BF16)
+        nc.sync.dma_start(
+            out=w_rows[:],
+            in_=target_matrix[HALF:, HALF:].rearrange("(s r) k -> r s k", r=P),
+        )
+        g_chunks = grad_out.rearrange("(c r t) d -> c r t d", r=P, t=ROWS_PER_PARTITION)
+        out_chunks = out.rearrange("(c r t) d -> c r t d", r=P, t=ROWS_PER_PARTITION)
+        g_tiles = []
+        for c in range(CHUNKS):
+            g_tile = loads.tile([P, ROWS_PER_PARTITION, DIM], BF16)
+            nc.sync.dma_start(out=g_tile[:], in_=g_chunks[c])
+            g_tiles.append(g_tile)
+
+        identity = const.tile([P, P], F32)
+        make_identity(nc, identity[:])
+
+        w_codes = const.tile([P, HALF], U32, align_bytes=64)
+        w_scales = const.tile([P, HALF], U8, align_bytes=64)
+        quantise_four_row_tiles(
+            nc, stage, flip_psum, identity[:], w_rows[:], w_codes[:], w_scales[:], E4M3_X4
+        )
+
+        for c in range(CHUNKS):
+            g_tile = g_tiles[c]
+            out_tile = results.tile([P, ROWS_PER_PARTITION, DIM], F32)
+            for first in range(0, ROWS_PER_PARTITION, QUAD):
+                four = slice(first, first + QUAD)
+                nc.vector.tensor_copy(out=out_tile[:, four, :HALF], in_=g_tile[:, four, :HALF])
+                g_codes = stage.tile([P, QUAD * P], U32, align_bytes=64)
+                g_scales = stage.tile([P, QUAD * P], U8, align_bytes=64)
+                quantise_four_row_tiles(
+                    nc,
+                    stage,
+                    flip_psum,
+                    identity[:],
+                    g_tile[:, four, HALF:],
+                    g_codes[:],
+                    g_scales[:],
+                    E5M2_X4,
+                )
+                for s in range(QUAD):
+                    row_tile = slice(s * P, (s + 1) * P)
+                    product = product_psum.tile([P, HALF], F32)
+                    nc.tensor.matmul_mx(
+                        out=product[:],
+                        lhsT=g_codes[:, row_tile].bitcast(E5M2_X4),
+                        lhsT_scale=g_scales[:, row_tile],
+                        rhs=w_codes[:].bitcast(E4M3_X4),
+                        rhs_scale=w_scales[:],
+                        start=True,
+                        stop=True,
+                    )
+                    nc.scalar.copy(out=out_tile[:, first + s, HALF:], in_=product[:])
+            nc.sync.dma_start(out=out_chunks[c], in_=out_tile[:])

@@ -19,7 +19,7 @@ HALF = DIM // 2
 QUAD = 4
 BANK_ROW_TILES = 2
 
-ROWS_PER_PARTITION = 8
+ROWS_PER_PARTITION = 4
 CHUNKS = BATCH // (P * ROWS_PER_PARTITION)
 
 FLOPS = 2 * BATCH * HALF * HALF

@@ -16,29 +16,35 @@ PAIR = 2
 BATCH = 4096
 DIM = 1024
 HALF = DIM // 2
+assert HALF == P * PACK
 QUAD = 4
 BANK_ROW_TILES = 2
+MX_ALIGN = 64
 
-ROWS_PER_PARTITION = 4
+ROWS_PER_PARTITION = 8
 CHUNKS = BATCH // (P * ROWS_PER_PARTITION)
+
+STAGE_BUFS = 3
+FLIP_BANKS = 4
+PRODUCT_BANKS = 4
 
 FLOPS = 2 * BATCH * HALF * HALF
 BYTES = BATCH * DIM * 2 + HALF * HALF * 2 + BATCH * DIM * 4
 
 
 def quantise_four_row_tiles(nc, stage, flip_psum, identity, rows, codes, scales, fp8_x4):
-    grouped = stage.tile([P, QUAD * P * PACK], BF16, align_bytes=64)
+    grouped = stage.tile([P, QUAD * P * PACK], BF16, align_bytes=MX_ALIGN)
     grouped_words = grouped[:].bitcast(F32).rearrange(
         "q (s r u) -> q s r u", s=QUAD, r=P, u=PAIR
     )
-    for first in range(0, QUAD, BANK_ROW_TILES):
+    for bank_first in range(0, QUAD, BANK_ROW_TILES):
         flipped = flip_psum.tile([P, BANK_ROW_TILES, PAIR, P], F32)
         for i in range(BANK_ROW_TILES):
-            words = rows[:, first + i, :].bitcast(F32).rearrange("r (q u) -> r u q", u=PAIR)
+            words = rows[:, bank_first + i, :].bitcast(F32).rearrange("r (q u) -> r u q", u=PAIR)
             for u in range(PAIR):
                 nc.tensor.transpose(flipped[:, i, u, :], words[:, u, :], identity)
         nc.vector.tensor_copy(
-            out=grouped_words[:, first : first + BANK_ROW_TILES, :, :],
+            out=grouped_words[:, bank_first : bank_first + BANK_ROW_TILES, :, :],
             in_=flipped[:].rearrange("q i u r -> q i r u"),
         )
     nc.vector.quantize_mx(out=codes.bitcast(fp8_x4), scales=scales, in_=grouped[:])
@@ -54,9 +60,9 @@ def tile_builtcontrolled_t_kernel(
         const = ctx.enter_context(tc.tile_pool(name="const", bufs=1))
         loads = ctx.enter_context(tc.tile_pool(name="loads", bufs=CHUNKS))
         results = ctx.enter_context(tc.tile_pool(name="results", bufs=CHUNKS))
-        stage = ctx.enter_context(tc.tile_pool(name="stage", bufs=3))
-        flip_psum = ctx.enter_context(tc.psum_pool(name="flip_psum", bufs=4))
-        product_psum = ctx.enter_context(tc.psum_pool(name="product_psum", bufs=4))
+        stage = ctx.enter_context(tc.tile_pool(name="stage", bufs=STAGE_BUFS))
+        flip_psum = ctx.enter_context(tc.psum_pool(name="flip_psum", bufs=FLIP_BANKS))
+        product_psum = ctx.enter_context(tc.psum_pool(name="product_psum", bufs=PRODUCT_BANKS))
 
         w_rows = const.tile([P, QUAD, HALF], BF16)
         nc.sync.dma_start(
@@ -74,8 +80,8 @@ def tile_builtcontrolled_t_kernel(
         identity = const.tile([P, P], F32)
         make_identity(nc, identity[:])
 
-        w_codes = const.tile([P, HALF], U32, align_bytes=64)
-        w_scales = const.tile([P, HALF], U8, align_bytes=64)
+        w_codes = const.tile([P, HALF], U32, align_bytes=MX_ALIGN)
+        w_scales = const.tile([P, HALF], U8, align_bytes=MX_ALIGN)
         quantise_four_row_tiles(
             nc, stage, flip_psum, identity[:], w_rows[:], w_codes[:], w_scales[:], E4M3_X4
         )
@@ -83,11 +89,10 @@ def tile_builtcontrolled_t_kernel(
         for c in range(CHUNKS):
             g_tile = g_tiles[c]
             out_tile = results.tile([P, ROWS_PER_PARTITION, DIM], F32)
-            for first in range(0, ROWS_PER_PARTITION, QUAD):
-                four = slice(first, first + QUAD)
-                nc.vector.tensor_copy(out=out_tile[:, four, :HALF], in_=g_tile[:, four, :HALF])
-                g_codes = stage.tile([P, QUAD * P], U32, align_bytes=64)
-                g_scales = stage.tile([P, QUAD * P], U8, align_bytes=64)
+            for quad_first in range(0, ROWS_PER_PARTITION, QUAD):
+                four = slice(quad_first, quad_first + QUAD)
+                g_codes = stage.tile([P, QUAD * P], U32, align_bytes=MX_ALIGN)
+                g_scales = stage.tile([P, QUAD * P], U8, align_bytes=MX_ALIGN)
                 quantise_four_row_tiles(
                     nc,
                     stage,
@@ -99,16 +104,17 @@ def tile_builtcontrolled_t_kernel(
                     E5M2_X4,
                 )
                 for s in range(QUAD):
-                    row_tile = slice(s * P, (s + 1) * P)
+                    code_cols = slice(s * P, (s + 1) * P)
                     product = product_psum.tile([P, HALF], F32)
                     nc.tensor.matmul_mx(
                         out=product[:],
-                        lhsT=g_codes[:, row_tile].bitcast(E5M2_X4),
-                        lhsT_scale=g_scales[:, row_tile],
+                        lhsT=g_codes[:, code_cols].bitcast(E5M2_X4),
+                        lhsT_scale=g_scales[:, code_cols],
                         rhs=w_codes[:].bitcast(E4M3_X4),
                         rhs_scale=w_scales[:],
                         start=True,
                         stop=True,
                     )
-                    nc.scalar.copy(out=out_tile[:, first + s, HALF:], in_=product[:])
+                    nc.scalar.copy(out=out_tile[:, quad_first + s, HALF:], in_=product[:])
+                nc.vector.tensor_copy(out=out_tile[:, four, :HALF], in_=g_tile[:, four, :HALF])
             nc.sync.dma_start(out=out_chunks[c], in_=out_tile[:])

@@ -32,19 +32,26 @@ FLOPS = 2 * BATCH * HALF * HALF
 BYTES = BATCH * DIM * 2 + HALF * HALF * 2 + BATCH * DIM * 4
 
 
-def quantise_four_row_tiles(nc, stage, flip_psum, identity, rows, codes, scales, fp8_x4):
-    grouped = stage.tile([P, QUAD * P * PACK], BF16, align_bytes=MX_ALIGN)
-    grouped_words = grouped[:].bitcast(F32).rearrange(
-        "q (s r u) -> q s r u", s=QUAD, r=P, u=PAIR
-    )
+def transpose_four_row_tiles(nc, flip_psum, identity, rows):
+    banks = []
     for bank_first in range(0, QUAD, BANK_ROW_TILES):
         flipped = flip_psum.tile([P, BANK_ROW_TILES, PAIR, P], F32)
         for i in range(BANK_ROW_TILES):
             words = rows[:, bank_first + i, :].bitcast(F32).rearrange("r (q u) -> r u q", u=PAIR)
             for u in range(PAIR):
                 nc.tensor.transpose(flipped[:, i, u, :], words[:, u, :], identity)
+        banks.append(flipped)
+    return banks
+
+
+def quantise_four_row_tiles(nc, stage, banks, codes, scales, fp8_x4):
+    grouped = stage.tile([P, QUAD * P * PACK], BF16, align_bytes=MX_ALIGN)
+    grouped_words = grouped[:].bitcast(F32).rearrange(
+        "q (s r u) -> q s r u", s=QUAD, r=P, u=PAIR
+    )
+    for b, flipped in enumerate(banks):
         nc.vector.tensor_copy(
-            out=grouped_words[:, bank_first : bank_first + BANK_ROW_TILES, :, :],
+            out=grouped_words[:, b * BANK_ROW_TILES : (b + 1) * BANK_ROW_TILES, :, :],
             in_=flipped[:].rearrange("q i u r -> q i r u"),
         )
     nc.vector.quantize_mx(out=codes.bitcast(fp8_x4), scales=scales, in_=grouped[:])
@@ -64,6 +71,11 @@ def tile_builtcontrolled_t_kernel(
         flip_psum = ctx.enter_context(tc.psum_pool(name="flip_psum", bufs=FLIP_BANKS))
         product_psum = ctx.enter_context(tc.psum_pool(name="product_psum", bufs=PRODUCT_BANKS))
 
+        identity = const.tile([P, P], F32)
+        make_identity(nc, identity[:])
+
+        ctx.enter_context(tc.manual_schedule())
+
         w_rows = const.tile([P, QUAD, HALF], BF16)
         nc.sync.dma_start(
             out=w_rows[:],
@@ -72,49 +84,54 @@ def tile_builtcontrolled_t_kernel(
         g_chunks = grad_out.rearrange("(c r t) d -> c r t d", r=P, t=ROWS_PER_PARTITION)
         out_chunks = out.rearrange("(c r t) d -> c r t d", r=P, t=ROWS_PER_PARTITION)
         g_tiles = []
+        out_tiles = []
         for c in range(CHUNKS):
             g_tile = loads.tile([P, ROWS_PER_PARTITION, DIM], BF16)
             nc.sync.dma_start(out=g_tile[:], in_=g_chunks[c])
             g_tiles.append(g_tile)
-
-        identity = const.tile([P, P], F32)
-        make_identity(nc, identity[:])
+            out_tile = results.tile([P, ROWS_PER_PARTITION, DIM], F32)
+            out_tiles.append(out_tile)
 
         w_codes = const.tile([P, HALF], U32, align_bytes=MX_ALIGN)
         w_scales = const.tile([P, HALF], U8, align_bytes=MX_ALIGN)
-        quantise_four_row_tiles(
-            nc, stage, flip_psum, identity[:], w_rows[:], w_codes[:], w_scales[:], E4M3_X4
-        )
+        w_banks = transpose_four_row_tiles(nc, flip_psum, identity[:], w_rows[:])
+        quantise_four_row_tiles(nc, stage, w_banks, w_codes[:], w_scales[:], E4M3_X4)
 
-        for c in range(CHUNKS):
-            g_tile = g_tiles[c]
-            out_tile = results.tile([P, ROWS_PER_PARTITION, DIM], F32)
-            for quad_first in range(0, ROWS_PER_PARTITION, QUAD):
-                four = slice(quad_first, quad_first + QUAD)
-                g_codes = stage.tile([P, QUAD * P], U32, align_bytes=MX_ALIGN)
-                g_scales = stage.tile([P, QUAD * P], U8, align_bytes=MX_ALIGN)
-                quantise_four_row_tiles(
-                    nc,
-                    stage,
-                    flip_psum,
-                    identity[:],
-                    g_tile[:, four, HALF:],
-                    g_codes[:],
-                    g_scales[:],
-                    E5M2_X4,
+        quads = [
+            (c, quad_first)
+            for c in range(CHUNKS)
+            for quad_first in range(0, ROWS_PER_PARTITION, QUAD)
+        ]
+
+        def transpose_quad(i):
+            c, quad_first = quads[i]
+            return transpose_four_row_tiles(
+                nc, flip_psum, identity[:], g_tiles[c][:, quad_first : quad_first + QUAD, HALF:]
+            )
+
+        banks = transpose_quad(0)
+        for i, (c, quad_first) in enumerate(quads):
+            four = slice(quad_first, quad_first + QUAD)
+            g_codes = stage.tile([P, QUAD * P], U32, align_bytes=MX_ALIGN)
+            g_scales = stage.tile([P, QUAD * P], U8, align_bytes=MX_ALIGN)
+            quantise_four_row_tiles(nc, stage, banks, g_codes[:], g_scales[:], E5M2_X4)
+            if i + 1 < len(quads):
+                banks = transpose_quad(i + 1)
+            for s in range(QUAD):
+                code_cols = slice(s * P, (s + 1) * P)
+                product = product_psum.tile([P, HALF], F32)
+                nc.tensor.matmul_mx(
+                    out=product[:],
+                    lhsT=g_codes[:, code_cols].bitcast(E5M2_X4),
+                    lhsT_scale=g_scales[:, code_cols],
+                    rhs=w_codes[:].bitcast(E4M3_X4),
+                    rhs_scale=w_scales[:],
+                    start=True,
+                    stop=True,
                 )
-                for s in range(QUAD):
-                    code_cols = slice(s * P, (s + 1) * P)
-                    product = product_psum.tile([P, HALF], F32)
-                    nc.tensor.matmul_mx(
-                        out=product[:],
-                        lhsT=g_codes[:, code_cols].bitcast(E5M2_X4),
-                        lhsT_scale=g_scales[:, code_cols],
-                        rhs=w_codes[:].bitcast(E4M3_X4),
-                        rhs_scale=w_scales[:],
-                        start=True,
-                        stop=True,
-                    )
-                    nc.scalar.copy(out=out_tile[:, quad_first + s, HALF:], in_=product[:])
-                nc.vector.tensor_copy(out=out_tile[:, four, :HALF], in_=g_tile[:, four, :HALF])
-            nc.sync.dma_start(out=out_chunks[c], in_=out_tile[:])
+                nc.scalar.copy(out=out_tiles[c][:, quad_first + s, HALF:], in_=product[:])
+            nc.vector.tensor_copy(out=out_tiles[c][:, four, :HALF], in_=g_tiles[c][:, four, :HALF])
+            if c == 0:
+                nc.sync.dma_start(out=out_chunks[c][:, four, :], in_=out_tiles[c][:, four, :])
+            elif quad_first + QUAD == ROWS_PER_PARTITION:
+                nc.sync.dma_start(out=out_chunks[c], in_=out_tiles[c][:])

@@ -131,7 +131,7 @@ def tile_builtcontrolled_t_kernel(
                 )
                 nc.scalar.copy(out=out_tiles[c][:, quad_first + s, HALF:], in_=product[:])
             nc.vector.tensor_copy(out=out_tiles[c][:, four, :HALF], in_=g_tiles[c][:, four, :HALF])
-            if c == 0:
+            if c == 0 or c == CHUNKS - 1:
                 nc.sync.dma_start(out=out_chunks[c][:, four, :], in_=out_tiles[c][:, four, :])
             elif quad_first + QUAD == ROWS_PER_PARTITION:
                 nc.sync.dma_start(out=out_chunks[c], in_=out_tiles[c][:])

@@ -21,12 +21,15 @@ QUAD = 4
 BANK_ROW_TILES = 2
 MX_ALIGN = 64
 
-ROWS_PER_PARTITION = 8
+ROWS_PER_PARTITION = 16
 CHUNKS = BATCH // (P * ROWS_PER_PARTITION)
 
 STAGE_BUFS = 3
 FLIP_BANKS = 4
 PRODUCT_BANKS = 4
+
+STORE_QUADS = (1, 1, 2, 2, 1, 1)
+assert sum(STORE_QUADS) * QUAD * P == BATCH
 
 FLOPS = 2 * BATCH * HALF * HALF
 BYTES = BATCH * DIM * 2 + HALF * HALF * 2 + BATCH * DIM * 4
@@ -103,6 +106,12 @@ def tile_builtcontrolled_t_kernel(
             for quad_first in range(0, ROWS_PER_PARTITION, QUAD)
         ]
 
+        first_quad_of_store = {}
+        stored = 0
+        for n in STORE_QUADS:
+            first_quad_of_store[stored + n - 1] = stored
+            stored += n
+
         def transpose_quad(i):
             c, quad_first = quads[i]
             return transpose_four_row_tiles(
@@ -131,7 +140,8 @@ def tile_builtcontrolled_t_kernel(
                 )
                 nc.scalar.copy(out=out_tiles[c][:, quad_first + s, HALF:], in_=product[:])
             nc.vector.tensor_copy(out=out_tiles[c][:, four, :HALF], in_=g_tiles[c][:, four, :HALF])
-            if c == 0 or c == CHUNKS - 1:
-                nc.sync.dma_start(out=out_chunks[c][:, four, :], in_=out_tiles[c][:, four, :])
-            elif quad_first + QUAD == ROWS_PER_PARTITION:
-                nc.sync.dma_start(out=out_chunks[c], in_=out_tiles[c][:])
+            if i in first_quad_of_store:
+                first_c, first_row = quads[first_quad_of_store[i]]
+                assert first_c == c
+                rows = slice(first_row, quad_first + QUAD)
+                nc.sync.dma_start(out=out_chunks[c][:, rows, :], in_=out_tiles[c][:, rows, :])

@@ -19,6 +19,7 @@ HALF = DIM // 2
 assert HALF == P * PACK
 QUAD = 4
 BANK_ROW_TILES = 2
+DMA_ALIGN = 4096
 MX_ALIGN = 64
 
 ROWS_PER_PARTITION = 16
@@ -79,7 +80,7 @@ def tile_builtcontrolled_t_kernel(
 
         ctx.enter_context(tc.manual_schedule())
 
-        w_rows = const.tile([P, QUAD, HALF], BF16)
+        w_rows = const.tile([P, QUAD, HALF], BF16, align_bytes=DMA_ALIGN)
         nc.sync.dma_start(
             out=w_rows[:],
             in_=target_matrix[HALF:, HALF:].rearrange("(s r) k -> r s k", r=P),
@@ -89,10 +90,10 @@ def tile_builtcontrolled_t_kernel(
         g_tiles = []
         out_tiles = []
         for c in range(CHUNKS):
-            g_tile = loads.tile([P, ROWS_PER_PARTITION, DIM], BF16)
+            g_tile = loads.tile([P, ROWS_PER_PARTITION, DIM], BF16, align_bytes=DMA_ALIGN)
             nc.sync.dma_start(out=g_tile[:], in_=g_chunks[c])
             g_tiles.append(g_tile)
-            out_tile = results.tile([P, ROWS_PER_PARTITION, DIM], F32)
+            out_tile = results.tile([P, ROWS_PER_PARTITION, DIM], F32, align_bytes=DMA_ALIGN)
             out_tiles.append(out_tile)
 
         w_codes = const.tile([P, HALF], U32, align_bytes=MX_ALIGN)

@@ -29,7 +29,7 @@ STAGE_BUFS = 3
 FLIP_BANKS = 4
 PRODUCT_BANKS = 4
 
-STORE_QUADS = (1, 1, 2, 2, 1, 1)
+STORE_QUADS = (1, 1, 2, 2, 2)
 assert sum(STORE_QUADS) * QUAD * P == BATCH
 
 FLOPS = 2 * BATCH * HALF * HALF

@@ -29,7 +29,7 @@ STAGE_BUFS = 3
 FLIP_BANKS = 4
 PRODUCT_BANKS = 4
 
-STORE_QUADS = (1, 1, 2, 2, 2)
+STORE_QUADS = (2, 2, 2, 2)
 assert sum(STORE_QUADS) * QUAD * P == BATCH
 
 FLOPS = 2 * BATCH * HALF * HALF

@@ -18,12 +18,13 @@ DIM = 1024
 HALF = DIM // 2
 assert HALF == P * PACK
 QUAD = 4
+QUADS = BATCH // (QUAD * P)
 BANK_ROW_TILES = 2
 DMA_ALIGN = 4096
 MX_ALIGN = 64
 
-ROWS_PER_PARTITION = 16
-CHUNKS = BATCH // (P * ROWS_PER_PARTITION)
+ROWS_PER_PARTITION = BATCH // P
+LOAD_QUADS = (3, 5)
 
 STAGE_BUFS = 3
 FLIP_BANKS = 4
@@ -69,8 +70,8 @@ def tile_builtcontrolled_t_kernel(
 
     with ExitStack() as ctx:
         const = ctx.enter_context(tc.tile_pool(name="const", bufs=1))
-        loads = ctx.enter_context(tc.tile_pool(name="loads", bufs=CHUNKS))
-        results = ctx.enter_context(tc.tile_pool(name="results", bufs=CHUNKS))
+        loads = ctx.enter_context(tc.tile_pool(name="loads", bufs=1))
+        results = ctx.enter_context(tc.tile_pool(name="results", bufs=1))
         stage = ctx.enter_context(tc.tile_pool(name="stage", bufs=STAGE_BUFS))
         flip_psum = ctx.enter_context(tc.psum_pool(name="flip_psum", bufs=FLIP_BANKS))
         product_psum = ctx.enter_context(tc.psum_pool(name="product_psum", bufs=PRODUCT_BANKS))
@@ -85,27 +86,20 @@ def tile_builtcontrolled_t_kernel(
             out=w_rows[:],
             in_=target_matrix[HALF:, HALF:].rearrange("(s r) k -> r s k", r=P),
         )
-        g_chunks = grad_out.rearrange("(c r t) d -> c r t d", r=P, t=ROWS_PER_PARTITION)
-        out_chunks = out.rearrange("(c r t) d -> c r t d", r=P, t=ROWS_PER_PARTITION)
-        g_tiles = []
-        out_tiles = []
-        for c in range(CHUNKS):
-            g_tile = loads.tile([P, ROWS_PER_PARTITION, DIM], BF16, align_bytes=DMA_ALIGN)
-            nc.sync.dma_start(out=g_tile[:], in_=g_chunks[c])
-            g_tiles.append(g_tile)
-            out_tile = results.tile([P, ROWS_PER_PARTITION, DIM], F32, align_bytes=DMA_ALIGN)
-            out_tiles.append(out_tile)
+        g_rows = grad_out.rearrange("(r t) d -> r t d", r=P)
+        out_rows = out.rearrange("(r t) d -> r t d", r=P)
+        g_tile = loads.tile([P, ROWS_PER_PARTITION, DIM], BF16, align_bytes=DMA_ALIGN)
+        out_tile = results.tile([P, ROWS_PER_PARTITION, DIM], F32, align_bytes=DMA_ALIGN)
+        loaded = 0
+        for n in LOAD_QUADS:
+            rows = slice(loaded * QUAD, (loaded + n) * QUAD)
+            nc.sync.dma_start(out=g_tile[:, rows, :], in_=g_rows[:, rows, :])
+            loaded += n
 
         w_codes = const.tile([P, HALF], U32, align_bytes=MX_ALIGN)
         w_scales = const.tile([P, HALF], U8, align_bytes=MX_ALIGN)
         w_banks = transpose_four_row_tiles(nc, flip_psum, identity[:], w_rows[:])
         quantise_four_row_tiles(nc, stage, w_banks, w_codes[:], w_scales[:], E4M3_X4)
-
-        quads = [
-            (c, quad_first)
-            for c in range(CHUNKS)
-            for quad_first in range(0, ROWS_PER_PARTITION, QUAD)
-        ]
 
         first_quad_of_store = {}
         stored = 0
@@ -114,35 +108,44 @@ def tile_builtcontrolled_t_kernel(
             stored += n
 
         def transpose_quad(i):
-            c, quad_first = quads[i]
-            return transpose_four_row_tiles(
-                nc, flip_psum, identity[:], g_tiles[c][:, quad_first : quad_first + QUAD, HALF:]
-            )
+            four = slice(i * QUAD, (i + 1) * QUAD)
+            return transpose_four_row_tiles(nc, flip_psum, identity[:], g_tile[:, four, HALF:])
 
-        banks = transpose_quad(0)
-        for i, (c, quad_first) in enumerate(quads):
-            four = slice(quad_first, quad_first + QUAD)
-            g_codes = stage.tile([P, QUAD * P], U32, align_bytes=MX_ALIGN)
-            g_scales = stage.tile([P, QUAD * P], U8, align_bytes=MX_ALIGN)
-            quantise_four_row_tiles(nc, stage, banks, g_codes[:], g_scales[:], E5M2_X4)
-            if i + 1 < len(quads):
-                banks = transpose_quad(i + 1)
-            for s in range(QUAD):
-                code_cols = slice(s * P, (s + 1) * P)
-                product = product_psum.tile([P, HALF], F32)
-                nc.tensor.matmul_mx(
-                    out=product[:],
-                    lhsT=g_codes[:, code_cols].bitcast(E5M2_X4),
-                    lhsT_scale=g_scales[:, code_cols],
-                    rhs=w_codes[:].bitcast(E4M3_X4),
-                    rhs_scale=w_scales[:],
-                    start=True,
-                    stop=True,
-                )
-                nc.scalar.copy(out=out_tiles[c][:, quad_first + s, HALF:], in_=product[:])
-            nc.vector.tensor_copy(out=out_tiles[c][:, four, :HALF], in_=g_tiles[c][:, four, :HALF])
-            if i in first_quad_of_store:
-                first_c, first_row = quads[first_quad_of_store[i]]
-                assert first_c == c
-                rows = slice(first_row, quad_first + QUAD)
-                nc.sync.dma_start(out=out_chunks[c][:, rows, :], in_=out_tiles[c][:, rows, :])
+        banks = {i: transpose_quad(i) for i in range(2)}
+        for first in range(0, QUADS, 2):
+            pair = range(first, first + 2)
+            quantised = {}
+            for i in pair:
+                g_codes = stage.tile([P, QUAD * P], U32, align_bytes=MX_ALIGN)
+                g_scales = stage.tile([P, QUAD * P], U8, align_bytes=MX_ALIGN)
+                quantise_four_row_tiles(nc, stage, banks[i], g_codes[:], g_scales[:], E5M2_X4)
+                quantised[i] = (g_codes, g_scales)
+            for i in pair:
+                g_codes, g_scales = quantised[i]
+                for s in range(QUAD):
+                    code_cols = slice(s * P, (s + 1) * P)
+                    product = product_psum.tile([P, HALF], F32)
+                    nc.tensor.matmul_mx(
+                        out=product[:],
+                        lhsT=g_codes[:, code_cols].bitcast(E5M2_X4),
+                        lhsT_scale=g_scales[:, code_cols],
+                        rhs=w_codes[:].bitcast(E4M3_X4),
+                        rhs_scale=w_scales[:],
+                        start=True,
+                        stop=True,
+                    )
+                    product_out = out_tile[:, i * QUAD + s, HALF:]
+                    if i == pair[-1] and s == QUAD - 1:
+                        last_product = (product_out, product[:])
+                    else:
+                        nc.scalar.copy(out=product_out, in_=product[:])
+                if i + 2 < QUADS:
+                    banks[i + 2] = transpose_quad(i + 2)
+            for i in pair:
+                four = slice(i * QUAD, (i + 1) * QUAD)
+                nc.vector.tensor_copy(out=out_tile[:, four, :HALF], in_=g_tile[:, four, :HALF])
+            nc.vector.tensor_copy(out=last_product[0], in_=last_product[1])
+            for i in pair:
+                if i in first_quad_of_store:
+                    rows = slice(first_quad_of_store[i] * QUAD, (i + 1) * QUAD)
+                    nc.sync.dma_start(out=out_rows[:, rows, :], in_=out_tile[:, rows, :])

@@ -148,4 +148,5 @@ def tile_builtcontrolled_t_kernel(
             for i in pair:
                 if i in first_quad_of_store:
                     rows = slice(first_quad_of_store[i] * QUAD, (i + 1) * QUAD)
-                    nc.sync.dma_start(out=out_rows[:, rows, :], in_=out_tile[:, rows, :])
+                    queue = nc.scalar if i + 1 == QUADS else nc.sync
+                    queue.dma_start(out=out_rows[:, rows, :], in_=out_tile[:, rows, :])

from contextlib import ExitStack

import concourse.mybir as mybir
from concourse.masks import make_identity

BF16 = mybir.dt.bfloat16
F32 = mybir.dt.float32
U32 = mybir.dt.uint32
U8 = mybir.dt.uint8
E5M2_X4 = mybir.dt.float8_e5m2_x4
E4M3_X4 = mybir.dt.float8_e4m3fn_x4

P = 128
PACK = 4
PAIR = 2
BATCH = 4096
DIM = 1024
HALF = DIM // 2
assert HALF == P * PACK
QUAD = 4
QUADS = BATCH // (QUAD * P)
BANK_ROW_TILES = 2
DMA_ALIGN = 4096
MX_ALIGN = 64

ROWS_PER_PARTITION = BATCH // P
LOAD_QUADS = (3, 5)

STAGE_BUFS = 3
FLIP_BANKS = 4
PRODUCT_BANKS = 4

STORE_QUADS = (2, 2, 2, 2)
assert sum(STORE_QUADS) * QUAD * P == BATCH

FLOPS = 2 * BATCH * HALF * HALF
BYTES = BATCH * DIM * 2 + HALF * HALF * 2 + BATCH * DIM * 4


def transpose_four_row_tiles(nc, flip_psum, identity, rows):
    banks = []
    for bank_first in range(0, QUAD, BANK_ROW_TILES):
        flipped = flip_psum.tile([P, BANK_ROW_TILES, PAIR, P], F32)
        for i in range(BANK_ROW_TILES):
            words = rows[:, bank_first + i, :].bitcast(F32).rearrange("r (q u) -> r u q", u=PAIR)
            for u in range(PAIR):
                nc.tensor.transpose(flipped[:, i, u, :], words[:, u, :], identity)
        banks.append(flipped)
    return banks


def quantise_four_row_tiles(nc, stage, banks, codes, scales, fp8_x4):
    grouped = stage.tile([P, QUAD * P * PACK], BF16, align_bytes=MX_ALIGN)
    grouped_words = grouped[:].bitcast(F32).rearrange(
        "q (s r u) -> q s r u", s=QUAD, r=P, u=PAIR
    )
    for b, flipped in enumerate(banks):
        nc.vector.tensor_copy(
            out=grouped_words[:, b * BANK_ROW_TILES : (b + 1) * BANK_ROW_TILES, :, :],
            in_=flipped[:].rearrange("q i u r -> q i r u"),
        )
    nc.vector.quantize_mx(out=codes.bitcast(fp8_x4), scales=scales, in_=grouped[:])


def tile_builtcontrolled_t_kernel(
    tc, state, target_matrix, control, num_qubits, grad_out, out
):
    nc = tc.nc
    assert control == 0 and num_qubits == 10

    with ExitStack() as ctx:
        const = ctx.enter_context(tc.tile_pool(name="const", bufs=1))
        loads = ctx.enter_context(tc.tile_pool(name="loads", bufs=1))
        results = ctx.enter_context(tc.tile_pool(name="results", bufs=1))
        stage = ctx.enter_context(tc.tile_pool(name="stage", bufs=STAGE_BUFS))
        flip_psum = ctx.enter_context(tc.psum_pool(name="flip_psum", bufs=FLIP_BANKS))
        product_psum = ctx.enter_context(tc.psum_pool(name="product_psum", bufs=PRODUCT_BANKS))

        identity = const.tile([P, P], F32)
        make_identity(nc, identity[:])

        ctx.enter_context(tc.manual_schedule())

        w_rows = const.tile([P, QUAD, HALF], BF16, align_bytes=DMA_ALIGN)
        nc.sync.dma_start(
            out=w_rows[:],
            in_=target_matrix[HALF:, HALF:].rearrange("(s r) k -> r s k", r=P),
        )
        g_rows = grad_out.rearrange("(r t) d -> r t d", r=P)
        out_rows = out.rearrange("(r t) d -> r t d", r=P)
        g_tile = loads.tile([P, ROWS_PER_PARTITION, DIM], BF16, align_bytes=DMA_ALIGN)
        out_tile = results.tile([P, ROWS_PER_PARTITION, DIM], F32, align_bytes=DMA_ALIGN)
        loaded = 0
        for n in LOAD_QUADS:
            rows = slice(loaded * QUAD, (loaded + n) * QUAD)
            nc.sync.dma_start(out=g_tile[:, rows, :], in_=g_rows[:, rows, :])
            loaded += n

        w_codes = const.tile([P, HALF], U32, align_bytes=MX_ALIGN)
        w_scales = const.tile([P, HALF], U8, align_bytes=MX_ALIGN)
        w_banks = transpose_four_row_tiles(nc, flip_psum, identity[:], w_rows[:])
        quantise_four_row_tiles(nc, stage, w_banks, w_codes[:], w_scales[:], E4M3_X4)

        first_quad_of_store = {}
        stored = 0
        for n in STORE_QUADS:
            first_quad_of_store[stored + n - 1] = stored
            stored += n

        def transpose_quad(i):
            four = slice(i * QUAD, (i + 1) * QUAD)
            return transpose_four_row_tiles(nc, flip_psum, identity[:], g_tile[:, four, HALF:])

        banks = {i: transpose_quad(i) for i in range(2)}
        for first in range(0, QUADS, 2):
            pair = range(first, first + 2)
            quantised = {}
            for i in pair:
                g_codes = stage.tile([P, QUAD * P], U32, align_bytes=MX_ALIGN)
                g_scales = stage.tile([P, QUAD * P], U8, align_bytes=MX_ALIGN)
                quantise_four_row_tiles(nc, stage, banks[i], g_codes[:], g_scales[:], E5M2_X4)
                quantised[i] = (g_codes, g_scales)
            for i in pair:
                g_codes, g_scales = quantised[i]
                for s in range(QUAD):
                    code_cols = slice(s * P, (s + 1) * P)
                    product = product_psum.tile([P, HALF], F32)
                    nc.tensor.matmul_mx(
                        out=product[:],
                        lhsT=g_codes[:, code_cols].bitcast(E5M2_X4),
                        lhsT_scale=g_scales[:, code_cols],
                        rhs=w_codes[:].bitcast(E4M3_X4),
                        rhs_scale=w_scales[:],
                        start=True,
                        stop=True,
                    )
                    product_out = out_tile[:, i * QUAD + s, HALF:]
                    if i == pair[-1] and s == QUAD - 1:
                        last_product = (product_out, product[:])
                    else:
                        nc.scalar.copy(out=product_out, in_=product[:])
                if i + 2 < QUADS:
                    banks[i + 2] = transpose_quad(i + 2)
            for i in pair:
                four = slice(i * QUAD, (i + 1) * QUAD)
                nc.vector.tensor_copy(out=out_tile[:, four, :HALF], in_=g_tile[:, four, :HALF])
            nc.vector.tensor_copy(out=last_product[0], in_=last_product[1])
            for i in pair:
                if i in first_quad_of_store:
                    rows = slice(first_quad_of_store[i] * QUAD, (i + 1) * QUAD)
                    queue = nc.scalar if i + 1 == QUADS else nc.sync
                    queue.dma_start(out=out_rows[:, rows, :], in_=out_tile[:, rows, :])
